import numpy as np
import ml_dtypes


def mxq(x, axis, fmt="e4m3"):
    dtype, down = {"e4m3": (ml_dtypes.float8_e4m3fn, 7), "e5m2": (ml_dtypes.float8_e5m2, 14)}[fmt]
    v = np.moveaxis(np.asarray(x, np.float32).astype(ml_dtypes.bfloat16).astype(np.float64), axis, -1)
    blocks = v.reshape(v.shape[:-1] + (-1, 32))
    amax = np.abs(blocks).max(-1, keepdims=True)
    byte = np.maximum(np.where(amax > 0, np.frexp(amax)[1] - 1 + 127, 0) - down, 1)
    scale = np.exp2(byte - 127.0)
    codes = (blocks / scale).astype(np.float32).astype(dtype).astype(np.float64)
    return np.moveaxis((codes * scale).reshape(v.shape), -1, axis)


WIDE = False


def mx_kscale(k):
    if not WIDE:
        return np.ones(k)
    levels = np.array([10, -10, 5, -5, 0])
    a = np.random.permutation(np.resize(levels, k // 512 * 4)).reshape(k // 512, 4)
    idx = np.arange(k)
    return np.exp2(a[idx // 512, idx % 128 // 32])


BF16 = ml_dtypes.bfloat16


def bf(x):
    return np.asarray(x, np.float32).astype(BF16)


def f64(x):
    return np.asarray(x).astype(np.float64)


L, T, H, A, NH, CR, NKV, HD = 4, 4096, 512, 512, 4, 4, 2, 128
Q = T // CR
KV = NKV * HD
RMS_EPS = 1e-5


def setup_inputs():
    s = mx_kscale(H)
    return {"cross_out": bf(np.random.standard_normal((L, Q, H)) * 3.5 / np.sqrt(T)),
            "pooled": bf(np.random.standard_normal((L, Q, H)) / np.sqrt(CR)),
            "residual_gate": bf(1.0 + 0.3 * np.random.standard_normal(1)),
            "frozen_ln": bf((1.0 + 0.1 * np.random.standard_normal((L, H))) * s),
            "frozen_k_proj": bf(np.random.standard_normal((L, KV, H)) / np.sqrt(H) / s),
            "frozen_v_proj": bf(np.random.standard_normal((L, KV, H)) / np.sqrt(H) / s)}


def reference(cross_out, pooled, residual_gate, frozen_ln, frozen_k_proj, frozen_v_proj):
    gate = 1.0 / (1.0 + np.exp(-f64(residual_gate)))
    compressed = gate * f64(cross_out) + (1.0 - gate) * f64(pooled)
    var = np.mean(compressed * compressed, axis=-1, keepdims=True)
    normed = compressed / np.sqrt(var + RMS_EPS) * f64(frozen_ln)[:, None, :]
    nq = mxq(normed, 2, "e4m3")
    k_out = nq @ mxq(f64(frozen_k_proj), 2, "e4m3").transpose(0, 2, 1)
    v_out = nq @ mxq(f64(frozen_v_proj), 2, "e4m3").transpose(0, 2, 1)
    k_out = k_out.reshape(L, Q, NKV, HD).transpose(0, 2, 1, 3)
    v_out = v_out.reshape(L, Q, NKV, HD).transpose(0, 2, 1, 3)
    return k_out, v_out

@@ -1,0 +1,221 @@
+from contextlib import ExitStack
+
+import concourse.mybir as mybir
+from concourse.masks import make_identity
+
+F32 = mybir.dt.float32
+BF16 = mybir.dt.bfloat16
+U32 = mybir.dt.uint32
+U8 = mybir.dt.uint8
+FP8X4 = mybir.dt.float8_e4m3fn_x4
+ACT = mybir.ActivationFunctionType
+ALU = mybir.AluOpType
+
+P = 128
+LAYERS = 4
+ROWS = 1024
+FEATURES = 512
+PAIRS = FEATURES // 2
+HALVES = PAIRS // P
+HEADS = 2
+HEAD_DIM = 128
+OUT_COLS = 2 * HEADS * HEAD_DIM
+RMS_EPS = 1e-5
+
+BLOCK_TILES = 4
+BLOCK_ROWS = P * BLOCK_TILES
+BLOCKS_PER_LAYER = ROWS // BLOCK_ROWS
+BLOCKS = LAYERS * BLOCKS_PER_LAYER
+TILES = 2
+GROUPS_PER_BLOCK = BLOCK_TILES // TILES
+GROUPS = BLOCKS * GROUPS_PER_BLOCK
+GROUP_COLS = TILES * FEATURES
+
+FLOPS = 2 * LAYERS * ROWS * FEATURES * OUT_COLS
+
+
+def tile_qformerkvcompressor_pc_t_kernel(
+    tc, cross_out, pooled, residual_gate, frozen_ln, frozen_k_proj, frozen_v_proj, out_0, out_1
+):
+    nc = tc.nc
+    with ExitStack() as ctx:
+        const = ctx.enter_context(tc.tile_pool(name="const", bufs=1))
+        inputs = ctx.enter_context(tc.tile_pool(name="inputs", bufs=BLOCKS))
+        weights = ctx.enter_context(tc.tile_pool(name="weights", bufs=LAYERS))
+        work = ctx.enter_context(tc.tile_pool(name="work", bufs=3))
+        psum_t = ctx.enter_context(tc.psum_pool(name="psum_t", bufs=2))
+        psum_w = ctx.enter_context(tc.psum_pool(name="psum_w", bufs=2))
+        psum_acc = ctx.enter_context(tc.psum_pool(name="psum_acc", bufs=4))
+        ctx.enter_context(tc.manual_schedule())
+
+        cross_blocks = cross_out.rearrange("l (b p j) h -> (l b) p (j h)", p=P, j=BLOCK_TILES)
+        pooled_blocks = pooled.rearrange("l (b p j) h -> (l b) p (j h)", p=P, j=BLOCK_TILES)
+        cross_sb, pooled_sb, w_raw = [], [], []
+
+        def load_block(b):
+            pooled_sb.append(inputs.tile([P, BLOCK_TILES * FEATURES], BF16, name="pooled_sb"))
+            cross_sb.append(inputs.tile([P, BLOCK_TILES * FEATURES], BF16, name="cross_sb"))
+            nc.sync.dma_start(out=pooled_sb[b][:], in_=pooled_blocks[b])
+            nc.sync.dma_start(out=cross_sb[b][:], in_=cross_blocks[b])
+
+        def load_weights(layer):
+            w_raw.append(weights.tile([P, 2, HEADS, FEATURES], BF16, name="w_raw"))
+            nc.sync.dma_start(out=w_raw[layer][:, 0], in_=frozen_k_proj[layer].rearrange("(n d) k -> d n k", d=P))
+            nc.sync.dma_start(out=w_raw[layer][:, 1], in_=frozen_v_proj[layer].rearrange("(n d) k -> d n k", d=P))
+
+        gate_logit = const.tile([P, 1], BF16)
+        nc.sync.dma_start(out=gate_logit[:], in_=residual_gate.partition_broadcast(P))
+        load_block(0)
+        load_block(1)
+        gain = const.tile([P, LAYERS, FEATURES], BF16)
+        nc.sync.dma_start(
+            out=gain[:].rearrange("p l h -> p (l h)"), in_=frozen_ln.rearrange("l h -> (l h)").partition_broadcast(P)
+        )
+        for layer in range(LAYERS):
+            load_weights(layer)
+            load_block(2 + layer)
+        for b in range(2 + LAYERS, BLOCKS):
+            load_block(b)
+
+        ident = const.tile([P, P], F32)
+        make_identity(nc, ident[:])
+        eps = const.tile([P, 1], F32)
+        nc.vector.memset(eps[:], RMS_EPS)
+        gate = const.tile([P, 1], F32)
+        one_minus_gate = const.tile([P, 1], F32)
+        nc.scalar.activation(out=gate[:], in_=gate_logit[:], func=ACT.Sigmoid)
+        nc.scalar.activation(out=one_minus_gate[:], in_=gate_logit[:], func=ACT.Sigmoid, scale=-1.0)
+
+        scaled_pooled, fused, std, transposed, grouped, codes, scales, acc, result = {}, {}, {}, {}, {}, {}, {}, {}, {}
+        w_ps, w_grouped, w_codes, w_scales = {}, {}, {}, {}
+
+        def group_cols(s):
+            first = (s % GROUPS_PER_BLOCK) * GROUP_COLS
+            return slice(first, first + GROUP_COLS)
+
+        def scale_pooled(s):
+            scaled_pooled[s] = work.tile([P, GROUP_COLS], F32, name="scaled_pooled")
+            nc.vector.tensor_scalar_mul(
+                out=scaled_pooled[s][:], in0=pooled_sb[s // GROUPS_PER_BLOCK][:, group_cols(s)],
+                scalar1=one_minus_gate[:, 0:1],
+            )
+
+        def fuse(s):
+            fused[s] = work.tile([P, TILES, FEATURES], F32, name="fused")
+            nc.vector.scalar_tensor_tensor(
+                out=fused[s][:].rearrange("p j h -> p (j h)"), in0=cross_sb[s // GROUPS_PER_BLOCK][:, group_cols(s)],
+                scalar=gate[:, 0:1], in1=scaled_pooled[s][:], op0=ALU.mult, op1=ALU.add,
+            )
+
+        def row_statistics(s):
+            sum_sq = work.tile([P, TILES], F32, name="sum_sq")
+            for j in range(TILES):
+                squares = work.tile([P, FEATURES], BF16, name="squares", bufs=4)
+                nc.scalar.activation(out=squares[:], in_=fused[s][:, j], func=ACT.Square, accum_out=sum_sq[:, j : j + 1])
+            std[s] = work.tile([P, TILES], F32, name="std")
+            nc.scalar.activation(out=std[s][:], in_=sum_sq[:], func=ACT.Sqrt, bias=eps[:, 0:1], scale=1.0 / FEATURES)
+
+        def normalise_and_transpose(s):
+            layer = s // (GROUPS_PER_BLOCK * BLOCKS_PER_LAYER)
+            rstd = work.tile([P, TILES], F32, name="rstd")
+            nc.vector.reciprocal(out=rstd[:], in_=std[s][:])
+            normed = work.tile([P, TILES, FEATURES], BF16, name="normed")
+            transposed[s] = psum_t.tile([P, TILES, HALVES, P], F32, name="transposed")
+            for j in range(TILES):
+                nc.vector.scalar_tensor_tensor(
+                    out=normed[:, j], in0=fused[s][:, j], scalar=rstd[:, j : j + 1], in1=gain[:, layer],
+                    op0=ALU.mult, op1=ALU.mult,
+                )
+                for u in range(HALVES):
+                    nc.tensor.transpose(
+                        out=transposed[s][:, j, u, :], in_=normed[:, j].bitcast(F32)[:, u * P : (u + 1) * P],
+                        identity=ident[:],
+                    )
+
+        def regroup(s):
+            grouped[s] = work.tile([P, GROUP_COLS], BF16, name="grouped", align_bytes=64)
+            nc.scalar.copy(
+                out=grouped[s][:].bitcast(F32).rearrange("p (j r u) -> p j r u", j=TILES, u=HALVES),
+                in_=transposed[s][:].rearrange("p j u r -> p j r u"),
+            )
+
+        def quantise(s):
+            codes[s] = work.tile([P, TILES * P], U32, name="codes", align_bytes=64)
+            scales[s] = work.tile([P, TILES * P], U8, name="scales", align_bytes=64)
+            nc.vector.quantize_mx(out=codes[s][:].bitcast(FP8X4), scales=scales[s][:], in_=grouped[s][:])
+
+        def project(s):
+            layer = s // (GROUPS_PER_BLOCK * BLOCKS_PER_LAYER)
+            for j in range(TILES):
+                acc[s, j] = psum_acc.tile([P, OUT_COLS], F32, name="acc")
+                nc.tensor.matmul_mx(
+                    out=acc[s, j][:],
+                    lhsT=codes[s][:, j * P : (j + 1) * P].bitcast(FP8X4), lhsT_scale=scales[s][:, j * P : (j + 1) * P],
+                    rhs=w_codes[layer][:].bitcast(FP8X4), rhs_scale=w_scales[layer][:],
+                    start=True, stop=True,
+                )
+
+        def store(s):
+            b, part = divmod(s, GROUPS_PER_BLOCK)
+            if part == 0:
+                result[b] = work.tile([P, 2 * HEADS, BLOCK_TILES, HEAD_DIM], F32, name="result")
+            for j in range(TILES):
+                nc.scalar.copy(
+                    out=result[b][:, :, part * TILES + j, :], in_=acc[s, j][:].rearrange("p (a d) -> p a d", d=HEAD_DIM)
+                )
+            if part == GROUPS_PER_BLOCK - 1:
+                layer, block_in_layer = divmod(b, BLOCKS_PER_LAYER)
+                for kv, out in enumerate((out_0, out_1)):
+                    nc.sync.dma_start(
+                        out=out[layer].rearrange("n (b p j) d -> b p n (j d)", p=P, j=BLOCK_TILES)[block_in_layer],
+                        in_=result[b][:, kv * HEADS : (kv + 1) * HEADS].rearrange("p n j d -> p n (j d)"),
+                    )
+
+        def transpose_weights(layer):
+            for kv in range(2):
+                w_ps[layer, kv] = psum_w.tile([P, HEADS, HALVES, P], F32, name="w_ps")
+                for n in range(HEADS):
+                    for u in range(HALVES):
+                        nc.tensor.transpose(
+                            out=w_ps[layer, kv][:, n, u, :],
+                            in_=w_raw[layer][:, kv, n].bitcast(F32)[:, u * P : (u + 1) * P], identity=ident[:],
+                        )
+
+        def regroup_weights(layer):
+            w_grouped[layer] = weights.tile([P, 2, HEADS * FEATURES], BF16, name="w_grouped", bufs=2, align_bytes=64)
+            for kv in range(2):
+                nc.scalar.copy(
+                    out=w_grouped[layer][:, kv].bitcast(F32).rearrange("p (n d u) -> p n d u", n=HEADS, u=HALVES),
+                    in_=w_ps[layer, kv][:].rearrange("p n u d -> p n d u"),
+                )
+
+        def quantise_weights(layer):
+            w_codes[layer] = weights.tile([P, OUT_COLS], U32, name="w_codes", align_bytes=64)
+            w_scales[layer] = weights.tile([P, OUT_COLS], U8, name="w_scales", align_bytes=64)
+            nc.vector.quantize_mx(
+                out=w_codes[layer][:].bitcast(FP8X4), scales=w_scales[layer][:],
+                in_=w_grouped[layer][:].rearrange("p a c -> p (a c)"),
+            )
+
+        scale_pooled(0)
+        for s in range(GROUPS + 3):
+            if s < GROUPS:
+                fuse(s)
+            if s + 1 < GROUPS:
+                scale_pooled(s + 1)
+            if 0 <= s - 1 < LAYERS:
+                transpose_weights(s - 1)
+            if 0 <= s - 1 < GROUPS:
+                row_statistics(s - 1)
+                normalise_and_transpose(s - 1)
+            if 0 <= s - 2 < GROUPS:
+                regroup(s - 2)
+            if 0 <= s - 2 < LAYERS:
+                quantise_weights(s - 2)
+            if 0 <= s - 2 < GROUPS:
+                quantise(s - 2)
+                project(s - 2)
+            if 0 <= s - 1 < LAYERS:
+                regroup_weights(s - 1)
+            if 0 <= s - 3:
+                store(s - 3)

@@ -21,6 +21,7 @@ HEADS = 2
 HEAD_DIM = 128
 OUT_COLS = 2 * HEADS * HEAD_DIM
 RMS_EPS = 1e-5
+MAX_LOGIT = 30.0
 
 BLOCK_TILES = 4
 BLOCK_ROWS = P * BLOCK_TILES
@@ -52,11 +53,17 @@ def tile_qformerkvcompressor_pc_t_kernel(
         pooled_blocks = pooled.rearrange("l (b p j) h -> (l b) p (j h)", p=P, j=BLOCK_TILES)
         cross_sb, pooled_sb, w_raw = [], [], []
 
-        def load_block(b):
-            pooled_sb.append(inputs.tile([P, BLOCK_TILES * FEATURES], BF16, name="pooled_sb"))
-            cross_sb.append(inputs.tile([P, BLOCK_TILES * FEATURES], BF16, name="cross_sb"))
-            nc.sync.dma_start(out=pooled_sb[b][:], in_=pooled_blocks[b])
-            nc.sync.dma_start(out=cross_sb[b][:], in_=cross_blocks[b])
+        def group_cols(s):
+            first = (s % GROUPS_PER_BLOCK) * GROUP_COLS
+            return slice(first, first + GROUP_COLS)
+
+        def load_group(s):
+            b = s // GROUPS_PER_BLOCK
+            if s % GROUPS_PER_BLOCK == 0:
+                pooled_sb.append(inputs.tile([P, BLOCK_TILES * FEATURES], BF16, name="pooled_sb"))
+                cross_sb.append(inputs.tile([P, BLOCK_TILES * FEATURES], BF16, name="cross_sb"))
+            nc.sync.dma_start(out=pooled_sb[b][:, group_cols(s)], in_=pooled_blocks[b][:, group_cols(s)])
+            nc.sync.dma_start(out=cross_sb[b][:, group_cols(s)], in_=cross_blocks[b][:, group_cols(s)])
 
         def load_weights(layer):
             w_raw.append(weights.tile([P, 2, HEADS, FEATURES], BF16, name="w_raw"))
@@ -65,65 +72,63 @@ def tile_qformerkvcompressor_pc_t_kernel(
 
         gate_logit = const.tile([P, 1], BF16)
         nc.sync.dma_start(out=gate_logit[:], in_=residual_gate.partition_broadcast(P))
-        load_block(0)
-        load_block(1)
-        gain = const.tile([P, LAYERS, FEATURES], BF16)
-        nc.sync.dma_start(
-            out=gain[:].rearrange("p l h -> p (l h)"), in_=frozen_ln.rearrange("l h -> (l h)").partition_broadcast(P)
-        )
-        for layer in range(LAYERS):
-            load_weights(layer)
-            load_block(2 + layer)
-        for b in range(2 + LAYERS, BLOCKS):
-            load_block(b)
+        load_group(0)
+        gain = const.tile([P, LAYERS * FEATURES], BF16)
+        nc.sync.dma_start(out=gain[:], in_=frozen_ln.rearrange("l h -> (l h)").partition_broadcast(P))
+        for s in range(1, GROUPS):
+            load_group(s)
+            if s - 1 < LAYERS:
+                load_weights(s - 1)
 
         ident = const.tile([P, P], F32)
         make_identity(nc, ident[:])
         eps = const.tile([P, 1], F32)
         nc.vector.memset(eps[:], RMS_EPS)
-        gate = const.tile([P, 1], F32)
+        capped_logit = const.tile([P, 1], F32)
+        odds = const.tile([P, 1], F32)
+        odds_plus_one = const.tile([P, 1], F32)
         one_minus_gate = const.tile([P, 1], F32)
-        nc.scalar.activation(out=gate[:], in_=gate_logit[:], func=ACT.Sigmoid)
-        nc.scalar.activation(out=one_minus_gate[:], in_=gate_logit[:], func=ACT.Sigmoid, scale=-1.0)
+        nc.vector.tensor_scalar_min(out=capped_logit[:], in0=gate_logit[:], scalar1=MAX_LOGIT)
+        nc.scalar.activation(out=odds[:], in_=capped_logit[:], func=ACT.Exp)
+        nc.vector.tensor_scalar_add(out=odds_plus_one[:], in0=odds[:], scalar1=1.0)
+        nc.vector.reciprocal(out=one_minus_gate[:], in_=odds_plus_one[:])
+        scaled_gain = const.tile([P, LAYERS, FEATURES], F32)
 
-        scaled_pooled, fused, std, transposed, grouped, codes, scales, acc, result = {}, {}, {}, {}, {}, {}, {}, {}, {}
+        mixed, sum_sq, rstd, transposed, grouped, codes, scales, acc, result = {}, {}, {}, {}, {}, {}, {}, {}, {}
         w_ps, w_grouped, w_codes, w_scales = {}, {}, {}, {}
 
-        def group_cols(s):
-            first = (s % GROUPS_PER_BLOCK) * GROUP_COLS
-            return slice(first, first + GROUP_COLS)
-
-        def scale_pooled(s):
-            scaled_pooled[s] = work.tile([P, GROUP_COLS], F32, name="scaled_pooled")
-            nc.vector.tensor_scalar_mul(
-                out=scaled_pooled[s][:], in0=pooled_sb[s // GROUPS_PER_BLOCK][:, group_cols(s)],
-                scalar1=one_minus_gate[:, 0:1],
-            )
+        def layer_of(s):
+            return s // (GROUPS_PER_BLOCK * BLOCKS_PER_LAYER)
 
         def fuse(s):
-            fused[s] = work.tile([P, TILES, FEATURES], F32, name="fused")
+            b = s // GROUPS_PER_BLOCK
+            mixed[s] = work.tile([P, TILES, FEATURES], F32, name="mixed")
             nc.vector.scalar_tensor_tensor(
-                out=fused[s][:].rearrange("p j h -> p (j h)"), in0=cross_sb[s // GROUPS_PER_BLOCK][:, group_cols(s)],
-                scalar=gate[:, 0:1], in1=scaled_pooled[s][:], op0=ALU.mult, op1=ALU.add,
+                out=mixed[s][:].rearrange("p j h -> p (j h)"), in0=cross_sb[b][:, group_cols(s)], scalar=odds[:, 0:1],
+                in1=pooled_sb[b][:, group_cols(s)], op0=ALU.mult, op1=ALU.add,
             )
 
-        def row_statistics(s):
-            sum_sq = work.tile([P, TILES], F32, name="sum_sq")
+        def sum_squares(s):
+            sum_sq[s] = work.tile([P, TILES], F32, name="sum_sq")
             for j in range(TILES):
                 squares = work.tile([P, FEATURES], BF16, name="squares", bufs=4)
-                nc.scalar.activation(out=squares[:], in_=fused[s][:, j], func=ACT.Square, accum_out=sum_sq[:, j : j + 1])
-            std[s] = work.tile([P, TILES], F32, name="std")
-            nc.scalar.activation(out=std[s][:], in_=sum_sq[:], func=ACT.Sqrt, bias=eps[:, 0:1], scale=1.0 / FEATURES)
+                nc.scalar.activation(
+                    out=squares[:], in_=mixed[s][:, j], func=ACT.Square, scale=one_minus_gate[:, 0:1],
+                    accum_out=sum_sq[s][:, j : j + 1],
+                )
+
+        def reciprocal_rms(s):
+            rms = work.tile([P, TILES], F32, name="rms")
+            nc.scalar.activation(out=rms[:], in_=sum_sq[s][:], func=ACT.Sqrt, bias=eps[:, 0:1], scale=1.0 / FEATURES)
+            rstd[s] = work.tile([P, TILES], F32, name="rstd")
+            nc.vector.reciprocal(out=rstd[s][:], in_=rms[:])
 
         def normalise_and_transpose(s):
-            layer = s // (GROUPS_PER_BLOCK * BLOCKS_PER_LAYER)
-            rstd = work.tile([P, TILES], F32, name="rstd")
-            nc.vector.reciprocal(out=rstd[:], in_=std[s][:])
             normed = work.tile([P, TILES, FEATURES], BF16, name="normed")
             transposed[s] = psum_t.tile([P, TILES, HALVES, P], F32, name="transposed")
             for j in range(TILES):
                 nc.vector.scalar_tensor_tensor(
-                    out=normed[:, j], in0=fused[s][:, j], scalar=rstd[:, j : j + 1], in1=gain[:, layer],
+                    out=normed[:, j], in0=mixed[s][:, j], scalar=rstd[s][:, j : j + 1], in1=scaled_gain[:, layer_of(s)],
                     op0=ALU.mult, op1=ALU.mult,
                 )
                 for u in range(HALVES):
@@ -139,36 +144,32 @@ def tile_qformerkvcompressor_pc_t_kernel(
                 in_=transposed[s][:].rearrange("p j u r -> p j r u"),
             )
 
-        def quantise(s):
+        def quantise_and_project(s):
             codes[s] = work.tile([P, TILES * P], U32, name="codes", align_bytes=64)
             scales[s] = work.tile([P, TILES * P], U8, name="scales", align_bytes=64)
             nc.vector.quantize_mx(out=codes[s][:].bitcast(FP8X4), scales=scales[s][:], in_=grouped[s][:])
-
-        def project(s):
-            layer = s // (GROUPS_PER_BLOCK * BLOCKS_PER_LAYER)
             for j in range(TILES):
                 acc[s, j] = psum_acc.tile([P, OUT_COLS], F32, name="acc")
                 nc.tensor.matmul_mx(
                     out=acc[s, j][:],
                     lhsT=codes[s][:, j * P : (j + 1) * P].bitcast(FP8X4), lhsT_scale=scales[s][:, j * P : (j + 1) * P],
-                    rhs=w_codes[layer][:].bitcast(FP8X4), rhs_scale=w_scales[layer][:],
+                    rhs=w_codes[layer_of(s)][:].bitcast(FP8X4), rhs_scale=w_scales[layer_of(s)][:],
                     start=True, stop=True,
                 )
 
-        def store(s):
+        def copy_out(s, j):
             b, part = divmod(s, GROUPS_PER_BLOCK)
-            if part == 0:
+            if part == 0 and j == 0:
                 result[b] = work.tile([P, 2 * HEADS, BLOCK_TILES, HEAD_DIM], F32, name="result")
-            for j in range(TILES):
-                nc.scalar.copy(
-                    out=result[b][:, :, part * TILES + j, :], in_=acc[s, j][:].rearrange("p (a d) -> p a d", d=HEAD_DIM)
-                )
-            if part == GROUPS_PER_BLOCK - 1:
+            nc.scalar.copy(
+                out=result[b][:, :, part * TILES + j, :], in_=acc[s, j][:].rearrange("p (a d) -> p a d", d=HEAD_DIM)
+            )
+            if part == GROUPS_PER_BLOCK - 1 and j == TILES - 1:
                 layer, block_in_layer = divmod(b, BLOCKS_PER_LAYER)
                 for kv, out in enumerate((out_0, out_1)):
                     nc.sync.dma_start(
-                        out=out[layer].rearrange("n (b p j) d -> b p n (j d)", p=P, j=BLOCK_TILES)[block_in_layer],
-                        in_=result[b][:, kv * HEADS : (kv + 1) * HEADS].rearrange("p n j d -> p n (j d)"),
+                        out=out[layer].rearrange("n (b p i) d -> b p n (i d)", p=P, i=BLOCK_TILES)[block_in_layer],
+                        in_=result[b][:, kv * HEADS : (kv + 1) * HEADS].rearrange("p n i d -> p n (i d)"),
                     )
 
         def transpose_weights(layer):
@@ -183,8 +184,8 @@ def tile_qformerkvcompressor_pc_t_kernel(
 
         def regroup_weights(layer):
             w_grouped[layer] = weights.tile([P, 2, HEADS * FEATURES], BF16, name="w_grouped", bufs=2, align_bytes=64)
-            for kv in range(2):
-                nc.scalar.copy(
+            for kv, copy in enumerate((nc.scalar.copy, nc.vector.tensor_copy)):
+                copy(
                     out=w_grouped[layer][:, kv].bitcast(F32).rearrange("p (n d u) -> p n d u", n=HEADS, u=HALVES),
                     in_=w_ps[layer, kv][:].rearrange("p n u d -> p n d u"),
                 )
@@ -197,25 +198,31 @@ def tile_qformerkvcompressor_pc_t_kernel(
                 in_=w_grouped[layer][:].rearrange("p a c -> p (a c)"),
             )
 
-        scale_pooled(0)
-        for s in range(GROUPS + 3):
-            if s < GROUPS:
-                fuse(s)
-            if s + 1 < GROUPS:
-                scale_pooled(s + 1)
-            if 0 <= s - 1 < LAYERS:
-                transpose_weights(s - 1)
+        fuse(0)
+        nc.vector.tensor_scalar_mul(
+            out=scaled_gain[:].rearrange("p l h -> p (l h)"), in0=gain[:], scalar1=one_minus_gate[:, 0:1]
+        )
+        for s in range(GROUPS + 2):
+            if s < LAYERS:
+                transpose_weights(s)
             if 0 <= s - 1 < GROUPS:
-                row_statistics(s - 1)
                 normalise_and_transpose(s - 1)
-            if 0 <= s - 2 < GROUPS:
-                regroup(s - 2)
-            if 0 <= s - 2 < LAYERS:
-                quantise_weights(s - 2)
-            if 0 <= s - 2 < GROUPS:
-                quantise(s - 2)
-                project(s - 2)
+            if s + 1 < GROUPS:
+                fuse(s + 1)
+            if s < GROUPS:
+                sum_squares(s)
+            if 0 <= s - 2:
+                copy_out(s - 2, 0)
+            if s < GROUPS:
+                reciprocal_rms(s)
+            if 0 <= s - 1 < GROUPS:
+                regroup(s - 1)
             if 0 <= s - 1 < LAYERS:
-                regroup_weights(s - 1)
-            if 0 <= s - 3:
-                store(s - 3)
+                quantise_weights(s - 1)
+            if 0 <= s - 1 < GROUPS:
+                quantise_and_project(s - 1)
+            if 0 <= s - 2:
+                for j in range(1, TILES):
+                    copy_out(s - 2, j)
+            if s < LAYERS:
+                regroup_weights(s)

@@ -21,15 +21,12 @@ HEADS = 2
 HEAD_DIM = 128
 OUT_COLS = 2 * HEADS * HEAD_DIM
 RMS_EPS = 1e-5
-MAX_LOGIT = 30.0
+MAX_LOGIT = 20.0
 
-BLOCK_TILES = 4
-BLOCK_ROWS = P * BLOCK_TILES
-BLOCKS_PER_LAYER = ROWS // BLOCK_ROWS
-BLOCKS = LAYERS * BLOCKS_PER_LAYER
 TILES = 2
-GROUPS_PER_BLOCK = BLOCK_TILES // TILES
-GROUPS = BLOCKS * GROUPS_PER_BLOCK
+GROUP_ROWS = P * TILES
+GROUPS_PER_LAYER = ROWS // GROUP_ROWS
+GROUPS = LAYERS * GROUPS_PER_LAYER
 GROUP_COLS = TILES * FEATURES
 
 FLOPS = 2 * LAYERS * ROWS * FEATURES * OUT_COLS
@@ -41,7 +38,7 @@ def tile_qformerkvcompressor_pc_t_kernel(
     nc = tc.nc
     with ExitStack() as ctx:
         const = ctx.enter_context(tc.tile_pool(name="const", bufs=1))
-        inputs = ctx.enter_context(tc.tile_pool(name="inputs", bufs=BLOCKS))
+        inputs = ctx.enter_context(tc.tile_pool(name="inputs", bufs=GROUPS))
         weights = ctx.enter_context(tc.tile_pool(name="weights", bufs=LAYERS))
         work = ctx.enter_context(tc.tile_pool(name="work", bufs=3))
         psum_t = ctx.enter_context(tc.psum_pool(name="psum_t", bufs=2))
@@ -49,77 +46,72 @@ def tile_qformerkvcompressor_pc_t_kernel(
         psum_acc = ctx.enter_context(tc.psum_pool(name="psum_acc", bufs=4))
         ctx.enter_context(tc.manual_schedule())
 
-        cross_blocks = cross_out.rearrange("l (b p j) h -> (l b) p (j h)", p=P, j=BLOCK_TILES)
-        pooled_blocks = pooled.rearrange("l (b p j) h -> (l b) p (j h)", p=P, j=BLOCK_TILES)
+        cross_groups = cross_out.rearrange("l (g p j) h -> (l g) p (j h)", p=P, j=TILES)
+        pooled_groups = pooled.rearrange("l (g p j) h -> (l g) p (j h)", p=P, j=TILES)
         cross_sb, pooled_sb, w_raw = [], [], []
-
-        def group_cols(s):
-            first = (s % GROUPS_PER_BLOCK) * GROUP_COLS
-            return slice(first, first + GROUP_COLS)
-
-        def load_group(s):
-            b = s // GROUPS_PER_BLOCK
-            if s % GROUPS_PER_BLOCK == 0:
-                pooled_sb.append(inputs.tile([P, BLOCK_TILES * FEATURES], BF16, name="pooled_sb"))
-                cross_sb.append(inputs.tile([P, BLOCK_TILES * FEATURES], BF16, name="cross_sb"))
-            nc.sync.dma_start(out=pooled_sb[b][:, group_cols(s)], in_=pooled_blocks[b][:, group_cols(s)])
-            nc.sync.dma_start(out=cross_sb[b][:, group_cols(s)], in_=cross_blocks[b][:, group_cols(s)])
-
-        def load_weights(layer):
-            w_raw.append(weights.tile([P, 2, HEADS, FEATURES], BF16, name="w_raw"))
-            nc.sync.dma_start(out=w_raw[layer][:, 0], in_=frozen_k_proj[layer].rearrange("(n d) k -> d n k", d=P))
-            nc.sync.dma_start(out=w_raw[layer][:, 1], in_=frozen_v_proj[layer].rearrange("(n d) k -> d n k", d=P))
-
         gate_logit = const.tile([P, 1], BF16)
         nc.sync.dma_start(out=gate_logit[:], in_=residual_gate.partition_broadcast(P))
-        load_group(0)
-        gain = const.tile([P, LAYERS * FEATURES], BF16)
-        nc.sync.dma_start(out=gain[:], in_=frozen_ln.rearrange("l h -> (l h)").partition_broadcast(P))
-        for s in range(1, GROUPS):
-            load_group(s)
-            if s - 1 < LAYERS:
-                load_weights(s - 1)
+        gain_rows = const.tile([P, FEATURES], BF16)
+        nc.vector.memset(gain_rows[:], 0.0)
+        for s in range(GROUPS):
+            pooled_sb.append(inputs.tile([P, GROUP_COLS], BF16, name="pooled_sb"))
+            cross_sb.append(inputs.tile([P, GROUP_COLS], BF16, name="cross_sb"))
+            nc.sync.dma_start(out=pooled_sb[s][:], in_=pooled_groups[s])
+            nc.sync.dma_start(out=cross_sb[s][:], in_=cross_groups[s])
+            if s == 0:
+                nc.sync.dma_start(out=gain_rows[0:LAYERS, :], in_=frozen_ln)
+            if 0 <= s - 1 < LAYERS:
+                w_raw.append(weights.tile([P, 2, HEADS, FEATURES], BF16, name="w_raw"))
+                nc.sync.dma_start(out=w_raw[s - 1][:, 0], in_=frozen_k_proj[s - 1].rearrange("(n d) k -> d n k", d=P))
+                nc.sync.dma_start(out=w_raw[s - 1][:, 1], in_=frozen_v_proj[s - 1].rearrange("(n d) k -> d n k", d=P))
 
         ident = const.tile([P, P], F32)
+        ident_bf16 = const.tile([P, P], BF16)
+        make_identity(nc, ident_bf16[:])
         make_identity(nc, ident[:])
-        eps = const.tile([P, 1], F32)
-        nc.vector.memset(eps[:], RMS_EPS)
         capped_logit = const.tile([P, 1], F32)
         odds = const.tile([P, 1], F32)
         odds_plus_one = const.tile([P, 1], F32)
-        one_minus_gate = const.tile([P, 1], F32)
+        scaled_eps = const.tile([P, 1], F32)
         nc.vector.tensor_scalar_min(out=capped_logit[:], in0=gate_logit[:], scalar1=MAX_LOGIT)
         nc.scalar.activation(out=odds[:], in_=capped_logit[:], func=ACT.Exp)
         nc.vector.tensor_scalar_add(out=odds_plus_one[:], in0=odds[:], scalar1=1.0)
-        nc.vector.reciprocal(out=one_minus_gate[:], in_=odds_plus_one[:])
-        scaled_gain = const.tile([P, LAYERS, FEATURES], F32)
+        nc.vector.scalar_tensor_tensor(
+            out=scaled_eps[:], in0=odds_plus_one[:], scalar=RMS_EPS, in1=odds_plus_one[:], op0=ALU.mult, op1=ALU.mult
+        )
+        gain = const.tile([P, LAYERS, FEATURES], BF16)
+        gain_ps = []
 
-        mixed, sum_sq, rstd, transposed, grouped, codes, scales, acc, result = {}, {}, {}, {}, {}, {}, {}, {}, {}
-        w_ps, w_grouped, w_codes, w_scales = {}, {}, {}, {}
-
-        def layer_of(s):
-            return s // (GROUPS_PER_BLOCK * BLOCKS_PER_LAYER)
-
-        def fuse(s):
-            b = s // GROUPS_PER_BLOCK
-            mixed[s] = work.tile([P, TILES, FEATURES], F32, name="mixed")
-            nc.vector.scalar_tensor_tensor(
-                out=mixed[s][:].rearrange("p j h -> p (j h)"), in0=cross_sb[b][:, group_cols(s)], scalar=odds[:, 0:1],
-                in1=pooled_sb[b][:, group_cols(s)], op0=ALU.mult, op1=ALU.add,
-            )
-
-        def sum_squares(s):
-            sum_sq[s] = work.tile([P, TILES], F32, name="sum_sq")
-            for j in range(TILES):
-                squares = work.tile([P, FEATURES], BF16, name="squares", bufs=4)
-                nc.scalar.activation(
-                    out=squares[:], in_=mixed[s][:, j], func=ACT.Square, scale=one_minus_gate[:, 0:1],
-                    accum_out=sum_sq[s][:, j : j + 1],
+        def spread_gain():
+            for layer in range(LAYERS):
+                gain_ps.append(psum_acc.tile([P, FEATURES], F32, name="acc"))
+                nc.tensor.matmul(
+                    out=gain_ps[layer][:], lhsT=ident_bf16[:, layer : layer + 1].to_broadcast([P, P]), rhs=gain_rows[:],
+                    start=True, stop=True,
                 )
 
-        def reciprocal_rms(s):
+        def keep_gain():
+            for layer in range(LAYERS):
+                copy = nc.scalar.copy if layer % 2 == 0 else nc.vector.tensor_copy
+                copy(out=gain[:, layer], in_=gain_ps[layer][:])
+
+        mixed, rstd, transposed, grouped, acc = {}, {}, {}, {}, {}
+        w_ps, w_grouped, w_codes, w_scales = {}, {}, {}, {}
+
+        def fuse(s):
+            mixed[s] = work.tile([P, TILES, FEATURES], F32, name="mixed")
+            nc.vector.scalar_tensor_tensor(
+                out=mixed[s][:].rearrange("p j h -> p (j h)"), in0=cross_sb[s][:], scalar=odds[:, 0:1],
+                in1=pooled_sb[s][:], op0=ALU.mult, op1=ALU.add,
+            )
+
+        def statistics(s):
+            sum_sq = work.tile([P, TILES], F32, name="sum_sq")
+            for j in range(TILES):
+                squares = work.tile([P, FEATURES], BF16, name="squares", bufs=4)
+                nc.scalar.activation(out=squares[:], in_=mixed[s][:, j], func=ACT.Square, accum_out=sum_sq[:, j : j + 1])
             rms = work.tile([P, TILES], F32, name="rms")
-            nc.scalar.activation(out=rms[:], in_=sum_sq[s][:], func=ACT.Sqrt, bias=eps[:, 0:1], scale=1.0 / FEATURES)
+            nc.scalar.activation(out=rms[:], in_=sum_sq[:], func=ACT.Sqrt, bias=scaled_eps[:, 0:1], scale=1.0 / FEATURES)
             rstd[s] = work.tile([P, TILES], F32, name="rstd")
             nc.vector.reciprocal(out=rstd[s][:], in_=rms[:])
 
@@ -128,7 +120,7 @@ def tile_qformerkvcompressor_pc_t_kernel(
             transposed[s] = psum_t.tile([P, TILES, HALVES, P], F32, name="transposed")
             for j in range(TILES):
                 nc.vector.scalar_tensor_tensor(
-                    out=normed[:, j], in0=mixed[s][:, j], scalar=rstd[s][:, j : j + 1], in1=scaled_gain[:, layer_of(s)],
+                    out=normed[:, j], in0=mixed[s][:, j], scalar=rstd[s][:, j : j + 1], in1=gain[:, s // GROUPS_PER_LAYER],
                     op0=ALU.mult, op1=ALU.mult,
                 )
                 for u in range(HALVES):
@@ -145,32 +137,30 @@ def tile_qformerkvcompressor_pc_t_kernel(
             )
 
         def quantise_and_project(s):
-            codes[s] = work.tile([P, TILES * P], U32, name="codes", align_bytes=64)
-            scales[s] = work.tile([P, TILES * P], U8, name="scales", align_bytes=64)
-            nc.vector.quantize_mx(out=codes[s][:].bitcast(FP8X4), scales=scales[s][:], in_=grouped[s][:])
+            layer = s // GROUPS_PER_LAYER
+            codes = work.tile([P, TILES * P], U32, name="codes", align_bytes=64)
+            scales = work.tile([P, TILES * P], U8, name="scales", align_bytes=64)
+            nc.vector.quantize_mx(out=codes[:].bitcast(FP8X4), scales=scales[:], in_=grouped[s][:])
             for j in range(TILES):
                 acc[s, j] = psum_acc.tile([P, OUT_COLS], F32, name="acc")
                 nc.tensor.matmul_mx(
                     out=acc[s, j][:],
-                    lhsT=codes[s][:, j * P : (j + 1) * P].bitcast(FP8X4), lhsT_scale=scales[s][:, j * P : (j + 1) * P],
-                    rhs=w_codes[layer_of(s)][:].bitcast(FP8X4), rhs_scale=w_scales[layer_of(s)][:],
+                    lhsT=codes[:, j * P : (j + 1) * P].bitcast(FP8X4), lhsT_scale=scales[:, j * P : (j + 1) * P],
+                    rhs=w_codes[layer][:].bitcast(FP8X4), rhs_scale=w_scales[layer][:],
                     start=True, stop=True,
                 )
 
-        def copy_out(s, j):
-            b, part = divmod(s, GROUPS_PER_BLOCK)
-            if part == 0 and j == 0:
-                result[b] = work.tile([P, 2 * HEADS, BLOCK_TILES, HEAD_DIM], F32, name="result")
-            nc.scalar.copy(
-                out=result[b][:, :, part * TILES + j, :], in_=acc[s, j][:].rearrange("p (a d) -> p a d", d=HEAD_DIM)
-            )
-            if part == GROUPS_PER_BLOCK - 1 and j == TILES - 1:
-                layer, block_in_layer = divmod(b, BLOCKS_PER_LAYER)
-                for kv, out in enumerate((out_0, out_1)):
-                    nc.sync.dma_start(
-                        out=out[layer].rearrange("n (b p i) d -> b p n (i d)", p=P, i=BLOCK_TILES)[block_in_layer],
-                        in_=result[b][:, kv * HEADS : (kv + 1) * HEADS].rearrange("p n i d -> p n (i d)"),
-                    )
+        def copy_out_and_store(s, vector_helps):
+            result = work.tile([P, 2 * HEADS, TILES, HEAD_DIM], F32, name="result")
+            for j in range(TILES):
+                copy = nc.vector.tensor_copy if vector_helps and j % 2 == 1 else nc.scalar.copy
+                copy(out=result[:, :, j, :], in_=acc[s, j][:].rearrange("p (a d) -> p a d", d=HEAD_DIM))
+            layer, part = divmod(s, GROUPS_PER_LAYER)
+            for kv, out in enumerate((out_0, out_1)):
+                nc.sync.dma_start(
+                    out=out[layer].rearrange("n (g p j) d -> g p n (j d)", p=P, j=TILES)[part],
+                    in_=result[:, kv * HEADS : (kv + 1) * HEADS].rearrange("p n j d -> p n (j d)"),
+                )
 
         def transpose_weights(layer):
             for kv in range(2):
@@ -199,30 +189,25 @@ def tile_qformerkvcompressor_pc_t_kernel(
             )
 
         fuse(0)
-        nc.vector.tensor_scalar_mul(
-            out=scaled_gain[:].rearrange("p l h -> p (l h)"), in0=gain[:], scalar1=one_minus_gate[:, 0:1]
-        )
+        spread_gain()
         for s in range(GROUPS + 2):
             if s < LAYERS:
                 transpose_weights(s)
+            if 0 <= s - 2:
+                regroup(s - 2)
             if 0 <= s - 1 < GROUPS:
                 normalise_and_transpose(s - 1)
+            if 0 <= s - 1 < LAYERS:
+                quantise_weights(s - 1)
+            if 0 <= s - 2:
+                quantise_and_project(s - 2)
             if s + 1 < GROUPS:
                 fuse(s + 1)
             if s < GROUPS:
-                sum_squares(s)
+                statistics(s)
+            if s == 0:
+                keep_gain()
             if 0 <= s - 2:
-                copy_out(s - 2, 0)
-            if s < GROUPS:
-                reciprocal_rms(s)
-            if 0 <= s - 1 < GROUPS:
-                regroup(s - 1)
-            if 0 <= s - 1 < LAYERS:
-                quantise_weights(s - 1)
-            if 0 <= s - 1 < GROUPS:
-                quantise_and_project(s - 1)
-            if 0 <= s - 2:
-                for j in range(1, TILES):
-                    copy_out(s - 2, j)
+                copy_out_and_store(s - 2, vector_helps=s + 1 >= GROUPS)
             if s < LAYERS:
                 regroup_weights(s)

@@ -151,7 +151,7 @@ def tile_qformerkvcompressor_pc_t_kernel(
                 )
 
         def copy_out_and_store(s, vector_helps):
-            result = work.tile([P, 2 * HEADS, TILES, HEAD_DIM], F32, name="result")
+            result = work.tile([P, 2 * HEADS, TILES, HEAD_DIM], F32, name="result", bufs=GROUPS)
             for j in range(TILES):
                 copy = nc.vector.tensor_copy if vector_helps and j % 2 == 1 else nc.scalar.copy
                 copy(out=result[:, :, j, :], in_=acc[s, j][:].rearrange("p (a d) -> p a d", d=HEAD_DIM))
@@ -190,16 +190,16 @@ def tile_qformerkvcompressor_pc_t_kernel(
 
         fuse(0)
         spread_gain()
-        for s in range(GROUPS + 2):
+        for s in range(GROUPS + 3):
             if s < LAYERS:
                 transpose_weights(s)
-            if 0 <= s - 2:
+            if 0 <= s - 2 < GROUPS:
                 regroup(s - 2)
             if 0 <= s - 1 < GROUPS:
                 normalise_and_transpose(s - 1)
             if 0 <= s - 1 < LAYERS:
                 quantise_weights(s - 1)
-            if 0 <= s - 2:
+            if 0 <= s - 2 < GROUPS:
                 quantise_and_project(s - 2)
             if s + 1 < GROUPS:
                 fuse(s + 1)
@@ -207,7 +207,7 @@ def tile_qformerkvcompressor_pc_t_kernel(
                 statistics(s)
             if s == 0:
                 keep_gain()
-            if 0 <= s - 2:
-                copy_out_and_store(s - 2, vector_helps=s + 1 >= GROUPS)
+            if 0 <= s - 3:
+                copy_out_and_store(s - 3, vector_helps=s + 1 >= GROUPS)
             if s < LAYERS:
                 regroup_weights(s)

@@ -110,10 +110,10 @@ def tile_qformerkvcompressor_pc_t_kernel(
             for j in range(TILES):
                 squares = work.tile([P, FEATURES], BF16, name="squares", bufs=4)
                 nc.scalar.activation(out=squares[:], in_=mixed[s][:, j], func=ACT.Square, accum_out=sum_sq[:, j : j + 1])
-            rms = work.tile([P, TILES], F32, name="rms")
-            nc.scalar.activation(out=rms[:], in_=sum_sq[:], func=ACT.Sqrt, bias=scaled_eps[:, 0:1], scale=1.0 / FEATURES)
             rstd[s] = work.tile([P, TILES], F32, name="rstd")
-            nc.vector.reciprocal(out=rstd[s][:], in_=rms[:])
+            nc.scalar.activation(
+                out=rstd[s][:], in_=sum_sq[:], func=ACT.Abs_reciprocal_sqrt, bias=scaled_eps[:, 0:1], scale=1.0 / FEATURES
+            )
 
         def normalise_and_transpose(s):
             normed = work.tile([P, TILES, FEATURES], BF16, name="normed")

@@ -23,11 +23,12 @@ OUT_COLS = 2 * HEADS * HEAD_DIM
 RMS_EPS = 1e-5
 MAX_LOGIT = 20.0
 
-TILES = 2
-GROUP_ROWS = P * TILES
-GROUPS_PER_LAYER = ROWS // GROUP_ROWS
-GROUPS = LAYERS * GROUPS_PER_LAYER
-GROUP_COLS = TILES * FEATURES
+GROUP_SIZES = ((1, 1, 2, 2, 2), (2, 2, 2, 2), (2, 2, 2, 2), (2, 2, 2, 1, 1))
+GROUP_LIST = [
+    (layer, P * sum(sizes[:i]), tiles) for layer, sizes in enumerate(GROUP_SIZES) for i, tiles in enumerate(sizes)
+]
+GROUPS = len(GROUP_LIST)
+SPLIT_GROUPS = 2
 
 FLOPS = 2 * LAYERS * ROWS * FEATURES * OUT_COLS
 
@@ -46,18 +47,20 @@ def tile_qformerkvcompressor_pc_t_kernel(
         psum_acc = ctx.enter_context(tc.psum_pool(name="psum_acc", bufs=4))
         ctx.enter_context(tc.manual_schedule())
 
-        cross_groups = cross_out.rearrange("l (g p j) h -> (l g) p (j h)", p=P, j=TILES)
-        pooled_groups = pooled.rearrange("l (g p j) h -> (l g) p (j h)", p=P, j=TILES)
+
+        def group_rows(rows, first_row, tiles):
+            return rows[first_row : first_row + P * tiles].rearrange("(p j) h -> p (j h)", j=tiles)
+
         cross_sb, pooled_sb, w_raw = [], [], []
         gate_logit = const.tile([P, 1], BF16)
         nc.sync.dma_start(out=gate_logit[:], in_=residual_gate.partition_broadcast(P))
         gain_rows = const.tile([P, FEATURES], BF16)
         nc.vector.memset(gain_rows[:], 0.0)
-        for s in range(GROUPS):
-            pooled_sb.append(inputs.tile([P, GROUP_COLS], BF16, name="pooled_sb"))
-            cross_sb.append(inputs.tile([P, GROUP_COLS], BF16, name="cross_sb"))
-            nc.sync.dma_start(out=pooled_sb[s][:], in_=pooled_groups[s])
-            nc.sync.dma_start(out=cross_sb[s][:], in_=cross_groups[s])
+        for s, (layer, first_row, tiles) in enumerate(GROUP_LIST):
+            pooled_sb.append(inputs.tile([P, tiles * FEATURES], BF16, name="pooled_sb"))
+            cross_sb.append(inputs.tile([P, tiles * FEATURES], BF16, name="cross_sb"))
+            nc.sync.dma_start(out=pooled_sb[s][:], in_=group_rows(pooled[layer], first_row, tiles))
+            nc.sync.dma_start(out=cross_sb[s][:], in_=group_rows(cross_out[layer], first_row, tiles))
             if s == 0:
                 nc.sync.dma_start(out=gain_rows[0:LAYERS, :], in_=frozen_ln)
             if 0 <= s - 1 < LAYERS:
@@ -75,52 +78,57 @@ def tile_qformerkvcompressor_pc_t_kernel(
         scaled_eps = const.tile([P, 1], F32)
         nc.vector.tensor_scalar_min(out=capped_logit[:], in0=gate_logit[:], scalar1=MAX_LOGIT)
         nc.scalar.activation(out=odds[:], in_=capped_logit[:], func=ACT.Exp)
+        table_loader = const.tile([P, 1], F32)
+        nc.scalar.activation(out=table_loader[:], in_=odds[:], func=ACT.Abs_reciprocal_sqrt)
         nc.vector.tensor_scalar_add(out=odds_plus_one[:], in0=odds[:], scalar1=1.0)
         nc.vector.scalar_tensor_tensor(
             out=scaled_eps[:], in0=odds_plus_one[:], scalar=RMS_EPS, in1=odds_plus_one[:], op0=ALU.mult, op1=ALU.mult
         )
+
         gain = const.tile([P, LAYERS, FEATURES], BF16)
-        gain_ps = []
+        gain_ps = {}
 
-        def spread_gain():
-            for layer in range(LAYERS):
-                gain_ps.append(psum_acc.tile([P, FEATURES], F32, name="acc"))
-                nc.tensor.matmul(
-                    out=gain_ps[layer][:], lhsT=ident_bf16[:, layer : layer + 1].to_broadcast([P, P]), rhs=gain_rows[:],
-                    start=True, stop=True,
-                )
+        def spread_gain(layer):
+            gain_ps[layer] = psum_w.tile([P, FEATURES], F32, name="w_ps")
+            nc.tensor.matmul(
+                out=gain_ps[layer][:], lhsT=ident_bf16[:, layer : layer + 1].to_broadcast([P, P]), rhs=gain_rows[:],
+                start=True, stop=True,
+            )
 
-        def keep_gain():
-            for layer in range(LAYERS):
-                copy = nc.scalar.copy if layer % 2 == 0 else nc.vector.tensor_copy
-                copy(out=gain[:, layer], in_=gain_ps[layer][:])
-
-        mixed, rstd, transposed, grouped, acc = {}, {}, {}, {}, {}
+        mixed, sum_sq, rstd, transposed, grouped, acc = {}, {}, {}, {}, {}, {}
         w_ps, w_grouped, w_codes, w_scales = {}, {}, {}, {}
 
         def fuse(s):
-            mixed[s] = work.tile([P, TILES, FEATURES], F32, name="mixed")
+            tiles = GROUP_LIST[s][2]
+            mixed[s] = work.tile([P, tiles, FEATURES], F32, name="mixed")
             nc.vector.scalar_tensor_tensor(
                 out=mixed[s][:].rearrange("p j h -> p (j h)"), in0=cross_sb[s][:], scalar=odds[:, 0:1],
                 in1=pooled_sb[s][:], op0=ALU.mult, op1=ALU.add,
             )
 
-        def statistics(s):
-            sum_sq = work.tile([P, TILES], F32, name="sum_sq")
-            for j in range(TILES):
+        def square(s):
+            tiles = GROUP_LIST[s][2]
+            sum_sq[s] = work.tile([P, tiles], F32, name="sum_sq")
+            for j in range(tiles):
                 squares = work.tile([P, FEATURES], BF16, name="squares", bufs=4)
-                nc.scalar.activation(out=squares[:], in_=mixed[s][:, j], func=ACT.Square, accum_out=sum_sq[:, j : j + 1])
-            rstd[s] = work.tile([P, TILES], F32, name="rstd")
+                nc.scalar.activation(
+                    out=squares[:], in_=mixed[s][:, j], func=ACT.Square, accum_out=sum_sq[s][:, j : j + 1]
+                )
+
+        def finish_statistics(s):
+            rstd[s] = work.tile([P, GROUP_LIST[s][2]], F32, name="rstd")
             nc.scalar.activation(
-                out=rstd[s][:], in_=sum_sq[:], func=ACT.Abs_reciprocal_sqrt, bias=scaled_eps[:, 0:1], scale=1.0 / FEATURES
+                out=rstd[s][:], in_=sum_sq[s][:], func=ACT.Abs_reciprocal_sqrt, bias=scaled_eps[:, 0:1],
+                scale=1.0 / FEATURES,
             )
 
         def normalise_and_transpose(s):
-            normed = work.tile([P, TILES, FEATURES], BF16, name="normed")
-            transposed[s] = psum_t.tile([P, TILES, HALVES, P], F32, name="transposed")
-            for j in range(TILES):
+            layer, first_row, tiles = GROUP_LIST[s]
+            normed = work.tile([P, tiles, FEATURES], BF16, name="normed")
+            transposed[s] = psum_t.tile([P, tiles, HALVES, P], F32, name="transposed")
+            for j in range(tiles):
                 nc.vector.scalar_tensor_tensor(
-                    out=normed[:, j], in0=mixed[s][:, j], scalar=rstd[s][:, j : j + 1], in1=gain[:, s // GROUPS_PER_LAYER],
+                    out=normed[:, j], in0=mixed[s][:, j], scalar=rstd[s][:, j : j + 1], in1=gain[:, layer],
                     op0=ALU.mult, op1=ALU.mult,
                 )
                 for u in range(HALVES):
@@ -130,35 +138,46 @@ def tile_qformerkvcompressor_pc_t_kernel(
                     )
 
         def regroup(s):
-            grouped[s] = work.tile([P, GROUP_COLS], BF16, name="grouped", align_bytes=64)
+            tiles = GROUP_LIST[s][2]
+            grouped[s] = work.tile([P, tiles * FEATURES], BF16, name="grouped", align_bytes=64)
             nc.scalar.copy(
-                out=grouped[s][:].bitcast(F32).rearrange("p (j r u) -> p j r u", j=TILES, u=HALVES),
+                out=grouped[s][:].bitcast(F32).rearrange("p (j r u) -> p j r u", j=tiles, u=HALVES),
                 in_=transposed[s][:].rearrange("p j u r -> p j r u"),
             )
 
         def quantise_and_project(s):
-            layer = s // GROUPS_PER_LAYER
-            codes = work.tile([P, TILES * P], U32, name="codes", align_bytes=64)
-            scales = work.tile([P, TILES * P], U8, name="scales", align_bytes=64)
+            layer, first_row, tiles = GROUP_LIST[s]
+            codes = work.tile([P, tiles * P], U32, name="codes", align_bytes=64)
+            scales = work.tile([P, tiles * P], U8, name="scales", align_bytes=64)
             nc.vector.quantize_mx(out=codes[:].bitcast(FP8X4), scales=scales[:], in_=grouped[s][:])
-            for j in range(TILES):
-                acc[s, j] = psum_acc.tile([P, OUT_COLS], F32, name="acc")
-                nc.tensor.matmul_mx(
-                    out=acc[s, j][:],
-                    lhsT=codes[:, j * P : (j + 1) * P].bitcast(FP8X4), lhsT_scale=scales[:, j * P : (j + 1) * P],
-                    rhs=w_codes[layer][:].bitcast(FP8X4), rhs_scale=w_scales[layer][:],
-                    start=True, stop=True,
-                )
+            banks = 2 if s >= GROUPS - SPLIT_GROUPS else 1
+            width = OUT_COLS // banks
+            for j in range(tiles):
+                for b in range(banks):
+                    acc[s, j, b] = psum_acc.tile([P, width], F32, name="acc")
+                    nc.tensor.matmul_mx(
+                        out=acc[s, j, b][:],
+                        lhsT=codes[:, j * P : (j + 1) * P].bitcast(FP8X4), lhsT_scale=scales[:, j * P : (j + 1) * P],
+                        rhs=w_codes[layer][:, b * width : (b + 1) * width].bitcast(FP8X4),
+                        rhs_scale=w_scales[layer][:, b * width : (b + 1) * width],
+                        start=True, stop=True,
+                    )
 
         def copy_out_and_store(s, vector_helps):
-            result = work.tile([P, 2 * HEADS, TILES, HEAD_DIM], F32, name="result", bufs=GROUPS)
-            for j in range(TILES):
-                copy = nc.vector.tensor_copy if vector_helps and j % 2 == 1 else nc.scalar.copy
-                copy(out=result[:, :, j, :], in_=acc[s, j][:].rearrange("p (a d) -> p a d", d=HEAD_DIM))
-            layer, part = divmod(s, GROUPS_PER_LAYER)
+            layer, first_row, tiles = GROUP_LIST[s]
+            result = work.tile([P, 2 * HEADS, tiles, HEAD_DIM], F32, name="result", bufs=GROUPS)
+            banks = 2 if s >= GROUPS - SPLIT_GROUPS else 1
+            heads = 2 * HEADS // banks
+            for j in range(tiles):
+                for b in range(banks):
+                    copy = nc.vector.tensor_copy if vector_helps and (j + b) % 2 == 1 else nc.scalar.copy
+                    copy(
+                        out=result[:, b * heads : (b + 1) * heads, j, :],
+                        in_=acc[s, j, b][:].rearrange("p (a d) -> p a d", d=HEAD_DIM),
+                    )
             for kv, out in enumerate((out_0, out_1)):
                 nc.sync.dma_start(
-                    out=out[layer].rearrange("n (g p j) d -> g p n (j d)", p=P, j=TILES)[part],
+                    out=out[layer][:, first_row : first_row + P * tiles].rearrange("n (p j) d -> p n (j d)", j=tiles),
                     in_=result[:, kv * HEADS : (kv + 1) * HEADS].rearrange("p n j d -> p n (j d)"),
                 )
 
@@ -189,25 +208,30 @@ def tile_qformerkvcompressor_pc_t_kernel(
             )
 
         fuse(0)
-        spread_gain()
-        for s in range(GROUPS + 3):
-            if s < LAYERS:
-                transpose_weights(s)
+        spread_gain(0)
+        nc.vector.tensor_copy(out=gain[:, 0], in_=gain_ps[0][:])
+        for s in range(GROUPS + 4):
+            if 0 <= s - 1 < LAYERS:
+                transpose_weights(s - 1)
+            if 0 < s - LAYERS < LAYERS:
+                spread_gain(s - LAYERS)
+            if 0 <= s - 4:
+                copy_out_and_store(s - 4, vector_helps=s + 1 >= GROUPS)
+            if s < GROUPS:
+                square(s)
             if 0 <= s - 2 < GROUPS:
                 regroup(s - 2)
+            if s < GROUPS:
+                finish_statistics(s)
+            if 0 <= s - 3 < LAYERS:
+                quantise_weights(s - 3)
+            if 0 <= s - 3 < GROUPS:
+                quantise_and_project(s - 3)
             if 0 <= s - 1 < GROUPS:
                 normalise_and_transpose(s - 1)
-            if 0 <= s - 1 < LAYERS:
-                quantise_weights(s - 1)
-            if 0 <= s - 2 < GROUPS:
-                quantise_and_project(s - 2)
             if s + 1 < GROUPS:
                 fuse(s + 1)
-            if s < GROUPS:
-                statistics(s)
-            if s == 0:
-                keep_gain()
-            if 0 <= s - 3:
-                copy_out_and_store(s - 3, vector_helps=s + 1 >= GROUPS)
-            if s < LAYERS:
-                regroup_weights(s)
+            if 0 <= s - 1 < LAYERS:
+                regroup_weights(s - 1)
+            if 0 < s - LAYERS < LAYERS:
+                nc.vector.tensor_copy(out=gain[:, s - LAYERS], in_=gain_ps[s - LAYERS][:])

@@ -28,6 +28,7 @@ GROUP_LIST = [
     (layer, P * sum(sizes[:i]), tiles) for layer, sizes in enumerate(GROUP_SIZES) for i, tiles in enumerate(sizes)
 ]
 GROUPS = len(GROUP_LIST)
+FIRST_GROUPS = {s: layer for s, (layer, first_row, tiles) in enumerate(GROUP_LIST) if first_row == 0}
 SPLIT_GROUPS = 2
 
 FLOPS = 2 * LAYERS * ROWS * FEATURES * OUT_COLS
@@ -63,10 +64,10 @@ def tile_qformerkvcompressor_pc_t_kernel(
             nc.sync.dma_start(out=cross_sb[s][:], in_=group_rows(cross_out[layer], first_row, tiles))
             if s == 0:
                 nc.sync.dma_start(out=gain_rows[0:LAYERS, :], in_=frozen_ln)
-            if 0 <= s - 1 < LAYERS:
+            if s - 1 in FIRST_GROUPS:
                 w_raw.append(weights.tile([P, 2, HEADS, FEATURES], BF16, name="w_raw"))
-                nc.sync.dma_start(out=w_raw[s - 1][:, 0], in_=frozen_k_proj[s - 1].rearrange("(n d) k -> d n k", d=P))
-                nc.sync.dma_start(out=w_raw[s - 1][:, 1], in_=frozen_v_proj[s - 1].rearrange("(n d) k -> d n k", d=P))
+                nc.sync.dma_start(out=w_raw[layer][:, 0], in_=frozen_k_proj[layer].rearrange("(n d) k -> d n k", d=P))
+                nc.sync.dma_start(out=w_raw[layer][:, 1], in_=frozen_v_proj[layer].rearrange("(n d) k -> d n k", d=P))
 
         ident = const.tile([P, P], F32)
         ident_bf16 = const.tile([P, P], BF16)
@@ -94,6 +95,9 @@ def tile_qformerkvcompressor_pc_t_kernel(
                 out=gain_ps[layer][:], lhsT=ident_bf16[:, layer : layer + 1].to_broadcast([P, P]), rhs=gain_rows[:],
                 start=True, stop=True,
             )
+
+        def keep_gain(layer):
+            nc.vector.tensor_copy(out=gain[:, layer], in_=gain_ps[layer][:])
 
         mixed, sum_sq, rstd, transposed, grouped, acc = {}, {}, {}, {}, {}, {}
         w_ps, w_grouped, w_codes, w_scales = {}, {}, {}, {}
@@ -209,12 +213,12 @@ def tile_qformerkvcompressor_pc_t_kernel(
 
         fuse(0)
         spread_gain(0)
-        nc.vector.tensor_copy(out=gain[:, 0], in_=gain_ps[0][:])
+        keep_gain(0)
         for s in range(GROUPS + 4):
-            if 0 <= s - 1 < LAYERS:
-                transpose_weights(s - 1)
-            if 0 < s - LAYERS < LAYERS:
-                spread_gain(s - LAYERS)
+            if s - 1 in FIRST_GROUPS:
+                transpose_weights(FIRST_GROUPS[s - 1])
+            if s > 0 and s in FIRST_GROUPS:
+                spread_gain(FIRST_GROUPS[s])
             if 0 <= s - 4:
                 copy_out_and_store(s - 4, vector_helps=s + 1 >= GROUPS)
             if s < GROUPS:
@@ -223,15 +227,15 @@ def tile_qformerkvcompressor_pc_t_kernel(
                 regroup(s - 2)
             if s < GROUPS:
                 finish_statistics(s)
-            if 0 <= s - 3 < LAYERS:
-                quantise_weights(s - 3)
+            if s - 3 in FIRST_GROUPS:
+                quantise_weights(FIRST_GROUPS[s - 3])
             if 0 <= s - 3 < GROUPS:
                 quantise_and_project(s - 3)
             if 0 <= s - 1 < GROUPS:
                 normalise_and_transpose(s - 1)
             if s + 1 < GROUPS:
                 fuse(s + 1)
-            if 0 <= s - 1 < LAYERS:
-                regroup_weights(s - 1)
-            if 0 < s - LAYERS < LAYERS:
-                nc.vector.tensor_copy(out=gain[:, s - LAYERS], in_=gain_ps[s - LAYERS][:])
+            if s - 1 in FIRST_GROUPS:
+                regroup_weights(FIRST_GROUPS[s - 1])
+            if s > 0 and s in FIRST_GROUPS:
+                keep_gain(FIRST_GROUPS[s])

@@ -90,14 +90,15 @@ def tile_qformerkvcompressor_pc_t_kernel(
         gain_ps = {}
 
         def spread_gain(layer):
-            gain_ps[layer] = psum_w.tile([P, FEATURES], F32, name="w_ps")
+            gain_ps[layer] = psum_w.tile([P, FEATURES], BF16, name="w_ps")
             nc.tensor.matmul(
                 out=gain_ps[layer][:], lhsT=ident_bf16[:, layer : layer + 1].to_broadcast([P, P]), rhs=gain_rows[:],
                 start=True, stop=True,
             )
 
         def keep_gain(layer):
-            nc.vector.tensor_copy(out=gain[:, layer], in_=gain_ps[layer][:])
+            copy = nc.vector.tensor_copy if layer == 0 else nc.scalar.copy
+            copy(out=gain[:, layer], in_=gain_ps[layer][:])
 
         mixed, sum_sq, rstd, transposed, grouped, acc = {}, {}, {}, {}, {}, {}
         w_ps, w_grouped, w_codes, w_scales = {}, {}, {}, {}
@@ -197,7 +198,8 @@ def tile_qformerkvcompressor_pc_t_kernel(
 
         def regroup_weights(layer):
             w_grouped[layer] = weights.tile([P, 2, HEADS * FEATURES], BF16, name="w_grouped", bufs=2, align_bytes=64)
-            for kv, copy in enumerate((nc.scalar.copy, nc.vector.tensor_copy)):
+            for kv in range(2):
+                copy = nc.scalar.copy if layer == 0 and kv == 0 else nc.vector.tensor_copy
                 copy(
                     out=w_grouped[layer][:, kv].bitcast(F32).rearrange("p (n d u) -> p n d u", n=HEADS, u=HALVES),
                     in_=w_ps[layer, kv][:].rearrange("p n u d -> p n d u"),
@@ -219,6 +221,10 @@ def tile_qformerkvcompressor_pc_t_kernel(
                 transpose_weights(FIRST_GROUPS[s - 1])
             if s > 0 and s in FIRST_GROUPS:
                 spread_gain(FIRST_GROUPS[s])
+            if s - 3 in FIRST_GROUPS:
+                quantise_weights(FIRST_GROUPS[s - 3])
+            if 0 <= s - 3 < GROUPS:
+                quantise_and_project(s - 3)
             if 0 <= s - 4:
                 copy_out_and_store(s - 4, vector_helps=s + 1 >= GROUPS)
             if s < GROUPS:
@@ -227,10 +233,6 @@ def tile_qformerkvcompressor_pc_t_kernel(
                 regroup(s - 2)
             if s < GROUPS:
                 finish_statistics(s)
-            if s - 3 in FIRST_GROUPS:
-                quantise_weights(FIRST_GROUPS[s - 3])
-            if 0 <= s - 3 < GROUPS:
-                quantise_and_project(s - 3)
             if 0 <= s - 1 < GROUPS:
                 normalise_and_transpose(s - 1)
             if s + 1 < GROUPS:

@@ -29,6 +29,7 @@ GROUP_LIST = [
 ]
 GROUPS = len(GROUP_LIST)
 FIRST_GROUPS = {s: layer for s, (layer, first_row, tiles) in enumerate(GROUP_LIST) if first_row == 0}
+SCALAR_LAYERS = 2
 SPLIT_GROUPS = 2
 
 FLOPS = 2 * LAYERS * ROWS * FEATURES * OUT_COLS
@@ -55,6 +56,7 @@ def tile_qformerkvcompressor_pc_t_kernel(
         cross_sb, pooled_sb, w_raw = [], [], []
         gate_logit = const.tile([P, 1], BF16)
         nc.sync.dma_start(out=gate_logit[:], in_=residual_gate.partition_broadcast(P))
+        gain = const.tile([P, LAYERS, FEATURES], BF16)
         gain_rows = const.tile([P, FEATURES], BF16)
         nc.vector.memset(gain_rows[:], 0.0)
         for s, (layer, first_row, tiles) in enumerate(GROUP_LIST):
@@ -64,6 +66,8 @@ def tile_qformerkvcompressor_pc_t_kernel(
             nc.sync.dma_start(out=cross_sb[s][:], in_=group_rows(cross_out[layer], first_row, tiles))
             if s == 0:
                 nc.sync.dma_start(out=gain_rows[0:LAYERS, :], in_=frozen_ln)
+            elif s in FIRST_GROUPS:
+                nc.sync.dma_start(out=gain[:, layer], in_=frozen_ln[layer].partition_broadcast(P))
             if s - 1 in FIRST_GROUPS:
                 w_raw.append(weights.tile([P, 2, HEADS, FEATURES], BF16, name="w_raw"))
                 nc.sync.dma_start(out=w_raw[layer][:, 0], in_=frozen_k_proj[layer].rearrange("(n d) k -> d n k", d=P))
@@ -86,19 +90,13 @@ def tile_qformerkvcompressor_pc_t_kernel(
             out=scaled_eps[:], in0=odds_plus_one[:], scalar=RMS_EPS, in1=odds_plus_one[:], op0=ALU.mult, op1=ALU.mult
         )
 
-        gain = const.tile([P, LAYERS, FEATURES], BF16)
-        gain_ps = {}
 
-        def spread_gain(layer):
-            gain_ps[layer] = psum_w.tile([P, FEATURES], BF16, name="w_ps")
+        def spread_first_gain():
+            gain_ps = psum_w.tile([P, FEATURES], BF16, name="w_ps")
             nc.tensor.matmul(
-                out=gain_ps[layer][:], lhsT=ident_bf16[:, layer : layer + 1].to_broadcast([P, P]), rhs=gain_rows[:],
-                start=True, stop=True,
+                out=gain_ps[:], lhsT=ident_bf16[:, 0:1].to_broadcast([P, P]), rhs=gain_rows[:], start=True, stop=True
             )
-
-        def keep_gain(layer):
-            copy = nc.vector.tensor_copy if layer == 0 else nc.scalar.copy
-            copy(out=gain[:, layer], in_=gain_ps[layer][:])
+            nc.vector.tensor_copy(out=gain[:, 0], in_=gain_ps[:])
 
         mixed, sum_sq, rstd, transposed, grouped, acc = {}, {}, {}, {}, {}, {}
         w_ps, w_grouped, w_codes, w_scales = {}, {}, {}, {}
@@ -199,7 +197,7 @@ def tile_qformerkvcompressor_pc_t_kernel(
         def regroup_weights(layer):
             w_grouped[layer] = weights.tile([P, 2, HEADS * FEATURES], BF16, name="w_grouped", bufs=2, align_bytes=64)
             for kv in range(2):
-                copy = nc.scalar.copy if layer == 0 and kv == 0 else nc.vector.tensor_copy
+                copy = nc.scalar.copy if layer < SCALAR_LAYERS and kv == 0 else nc.vector.tensor_copy
                 copy(
                     out=w_grouped[layer][:, kv].bitcast(F32).rearrange("p (n d u) -> p n d u", n=HEADS, u=HALVES),
                     in_=w_ps[layer, kv][:].rearrange("p n u d -> p n d u"),
@@ -214,13 +212,10 @@ def tile_qformerkvcompressor_pc_t_kernel(
             )
 
         fuse(0)
-        spread_gain(0)
-        keep_gain(0)
+        spread_first_gain()
         for s in range(GROUPS + 4):
             if s - 1 in FIRST_GROUPS:
                 transpose_weights(FIRST_GROUPS[s - 1])
-            if s > 0 and s in FIRST_GROUPS:
-                spread_gain(FIRST_GROUPS[s])
             if s - 3 in FIRST_GROUPS:
                 quantise_weights(FIRST_GROUPS[s - 3])
             if 0 <= s - 3 < GROUPS:
@@ -239,5 +234,3 @@ def tile_qformerkvcompressor_pc_t_kernel(
                 fuse(s + 1)
             if s - 1 in FIRST_GROUPS:
                 regroup_weights(FIRST_GROUPS[s - 1])
-            if s > 0 and s in FIRST_GROUPS:
-                keep_gain(FIRST_GROUPS[s])

@@ -29,7 +29,6 @@ GROUP_LIST = [
 ]
 GROUPS = len(GROUP_LIST)
 FIRST_GROUPS = {s: layer for s, (layer, first_row, tiles) in enumerate(GROUP_LIST) if first_row == 0}
-SCALAR_LAYERS = 2
 SPLIT_GROUPS = 2
 
 FLOPS = 2 * LAYERS * ROWS * FEATURES * OUT_COLS
@@ -195,9 +194,9 @@ def tile_qformerkvcompressor_pc_t_kernel(
                         )
 
         def regroup_weights(layer):
+            copy = nc.scalar.copy if layer == 0 else nc.vector.tensor_copy
             w_grouped[layer] = weights.tile([P, 2, HEADS * FEATURES], BF16, name="w_grouped", bufs=2, align_bytes=64)
             for kv in range(2):
-                copy = nc.scalar.copy if layer < SCALAR_LAYERS and kv == 0 else nc.vector.tensor_copy
                 copy(
                     out=w_grouped[layer][:, kv].bitcast(F32).rearrange("p (n d u) -> p n d u", n=HEADS, u=HALVES),
                     in_=w_ps[layer, kv][:].rearrange("p n u d -> p n d u"),

from contextlib import ExitStack

import concourse.mybir as mybir
from concourse.masks import make_identity

F32 = mybir.dt.float32
BF16 = mybir.dt.bfloat16
U32 = mybir.dt.uint32
U8 = mybir.dt.uint8
FP8X4 = mybir.dt.float8_e4m3fn_x4
ACT = mybir.ActivationFunctionType
ALU = mybir.AluOpType

P = 128
LAYERS = 4
ROWS = 1024
FEATURES = 512
PAIRS = FEATURES // 2
HALVES = PAIRS // P
HEADS = 2
HEAD_DIM = 128
OUT_COLS = 2 * HEADS * HEAD_DIM
RMS_EPS = 1e-5
MAX_LOGIT = 20.0

GROUP_SIZES = ((1, 1, 2, 2, 2), (2, 2, 2, 2), (2, 2, 2, 2), (2, 2, 2, 1, 1))
GROUP_LIST = [
    (layer, P * sum(sizes[:i]), tiles) for layer, sizes in enumerate(GROUP_SIZES) for i, tiles in enumerate(sizes)
]
GROUPS = len(GROUP_LIST)
FIRST_GROUPS = {s: layer for s, (layer, first_row, tiles) in enumerate(GROUP_LIST) if first_row == 0}
SPLIT_GROUPS = 2

FLOPS = 2 * LAYERS * ROWS * FEATURES * OUT_COLS


def tile_qformerkvcompressor_pc_t_kernel(
    tc, cross_out, pooled, residual_gate, frozen_ln, frozen_k_proj, frozen_v_proj, out_0, out_1
):
    nc = tc.nc
    with ExitStack() as ctx:
        const = ctx.enter_context(tc.tile_pool(name="const", bufs=1))
        inputs = ctx.enter_context(tc.tile_pool(name="inputs", bufs=GROUPS))
        weights = ctx.enter_context(tc.tile_pool(name="weights", bufs=LAYERS))
        work = ctx.enter_context(tc.tile_pool(name="work", bufs=3))
        psum_t = ctx.enter_context(tc.psum_pool(name="psum_t", bufs=2))
        psum_w = ctx.enter_context(tc.psum_pool(name="psum_w", bufs=2))
        psum_acc = ctx.enter_context(tc.psum_pool(name="psum_acc", bufs=4))
        ctx.enter_context(tc.manual_schedule())


        def group_rows(rows, first_row, tiles):
            return rows[first_row : first_row + P * tiles].rearrange("(p j) h -> p (j h)", j=tiles)

        cross_sb, pooled_sb, w_raw = [], [], []
        gate_logit = const.tile([P, 1], BF16)
        nc.sync.dma_start(out=gate_logit[:], in_=residual_gate.partition_broadcast(P))
        gain = const.tile([P, LAYERS, FEATURES], BF16)
        gain_rows = const.tile([P, FEATURES], BF16)
        nc.vector.memset(gain_rows[:], 0.0)
        for s, (layer, first_row, tiles) in enumerate(GROUP_LIST):
            pooled_sb.append(inputs.tile([P, tiles * FEATURES], BF16, name="pooled_sb"))
            cross_sb.append(inputs.tile([P, tiles * FEATURES], BF16, name="cross_sb"))
            nc.sync.dma_start(out=pooled_sb[s][:], in_=group_rows(pooled[layer], first_row, tiles))
            nc.sync.dma_start(out=cross_sb[s][:], in_=group_rows(cross_out[layer], first_row, tiles))
            if s == 0:
                nc.sync.dma_start(out=gain_rows[0:LAYERS, :], in_=frozen_ln)
            elif s in FIRST_GROUPS:
                nc.sync.dma_start(out=gain[:, layer], in_=frozen_ln[layer].partition_broadcast(P))
            if s - 1 in FIRST_GROUPS:
                w_raw.append(weights.tile([P, 2, HEADS, FEATURES], BF16, name="w_raw"))
                nc.sync.dma_start(out=w_raw[layer][:, 0], in_=frozen_k_proj[layer].rearrange("(n d) k -> d n k", d=P))
                nc.sync.dma_start(out=w_raw[layer][:, 1], in_=frozen_v_proj[layer].rearrange("(n d) k -> d n k", d=P))

        ident = const.tile([P, P], F32)
        ident_bf16 = const.tile([P, P], BF16)
        make_identity(nc, ident_bf16[:])
        make_identity(nc, ident[:])
        capped_logit = const.tile([P, 1], F32)
        odds = const.tile([P, 1], F32)
        odds_plus_one = const.tile([P, 1], F32)
        scaled_eps = const.tile([P, 1], F32)
        nc.vector.tensor_scalar_min(out=capped_logit[:], in0=gate_logit[:], scalar1=MAX_LOGIT)
        nc.scalar.activation(out=odds[:], in_=capped_logit[:], func=ACT.Exp)
        table_loader = const.tile([P, 1], F32)
        nc.scalar.activation(out=table_loader[:], in_=odds[:], func=ACT.Abs_reciprocal_sqrt)
        nc.vector.tensor_scalar_add(out=odds_plus_one[:], in0=odds[:], scalar1=1.0)
        nc.vector.scalar_tensor_tensor(
            out=scaled_eps[:], in0=odds_plus_one[:], scalar=RMS_EPS, in1=odds_plus_one[:], op0=ALU.mult, op1=ALU.mult
        )


        def spread_first_gain():
            gain_ps = psum_w.tile([P, FEATURES], BF16, name="w_ps")
            nc.tensor.matmul(
                out=gain_ps[:], lhsT=ident_bf16[:, 0:1].to_broadcast([P, P]), rhs=gain_rows[:], start=True, stop=True
            )
            nc.vector.tensor_copy(out=gain[:, 0], in_=gain_ps[:])

        mixed, sum_sq, rstd, transposed, grouped, acc = {}, {}, {}, {}, {}, {}
        w_ps, w_grouped, w_codes, w_scales = {}, {}, {}, {}

        def fuse(s):
            tiles = GROUP_LIST[s][2]
            mixed[s] = work.tile([P, tiles, FEATURES], F32, name="mixed")
            nc.vector.scalar_tensor_tensor(
                out=mixed[s][:].rearrange("p j h -> p (j h)"), in0=cross_sb[s][:], scalar=odds[:, 0:1],
                in1=pooled_sb[s][:], op0=ALU.mult, op1=ALU.add,
            )

        def square(s):
            tiles = GROUP_LIST[s][2]
            sum_sq[s] = work.tile([P, tiles], F32, name="sum_sq")
            for j in range(tiles):
                squares = work.tile([P, FEATURES], BF16, name="squares", bufs=4)
                nc.scalar.activation(
                    out=squares[:], in_=mixed[s][:, j], func=ACT.Square, accum_out=sum_sq[s][:, j : j + 1]
                )

        def finish_statistics(s):
            rstd[s] = work.tile([P, GROUP_LIST[s][2]], F32, name="rstd")
            nc.scalar.activation(
                out=rstd[s][:], in_=sum_sq[s][:], func=ACT.Abs_reciprocal_sqrt, bias=scaled_eps[:, 0:1],
                scale=1.0 / FEATURES,
            )

        def normalise_and_transpose(s):
            layer, first_row, tiles = GROUP_LIST[s]
            normed = work.tile([P, tiles, FEATURES], BF16, name="normed")
            transposed[s] = psum_t.tile([P, tiles, HALVES, P], F32, name="transposed")
            for j in range(tiles):
                nc.vector.scalar_tensor_tensor(
                    out=normed[:, j], in0=mixed[s][:, j], scalar=rstd[s][:, j : j + 1], in1=gain[:, layer],
                    op0=ALU.mult, op1=ALU.mult,
                )
                for u in range(HALVES):
                    nc.tensor.transpose(
                        out=transposed[s][:, j, u, :], in_=normed[:, j].bitcast(F32)[:, u * P : (u + 1) * P],
                        identity=ident[:],
                    )

        def regroup(s):
            tiles = GROUP_LIST[s][2]
            grouped[s] = work.tile([P, tiles * FEATURES], BF16, name="grouped", align_bytes=64)
            nc.scalar.copy(
                out=grouped[s][:].bitcast(F32).rearrange("p (j r u) -> p j r u", j=tiles, u=HALVES),
                in_=transposed[s][:].rearrange("p j u r -> p j r u"),
            )

        def quantise_and_project(s):
            layer, first_row, tiles = GROUP_LIST[s]
            codes = work.tile([P, tiles * P], U32, name="codes", align_bytes=64)
            scales = work.tile([P, tiles * P], U8, name="scales", align_bytes=64)
            nc.vector.quantize_mx(out=codes[:].bitcast(FP8X4), scales=scales[:], in_=grouped[s][:])
            banks = 2 if s >= GROUPS - SPLIT_GROUPS else 1
            width = OUT_COLS // banks
            for j in range(tiles):
                for b in range(banks):
                    acc[s, j, b] = psum_acc.tile([P, width], F32, name="acc")
                    nc.tensor.matmul_mx(
                        out=acc[s, j, b][:],
                        lhsT=codes[:, j * P : (j + 1) * P].bitcast(FP8X4), lhsT_scale=scales[:, j * P : (j + 1) * P],
                        rhs=w_codes[layer][:, b * width : (b + 1) * width].bitcast(FP8X4),
                        rhs_scale=w_scales[layer][:, b * width : (b + 1) * width],
                        start=True, stop=True,
                    )

        def copy_out_and_store(s, vector_helps):
            layer, first_row, tiles = GROUP_LIST[s]
            result = work.tile([P, 2 * HEADS, tiles, HEAD_DIM], F32, name="result", bufs=GROUPS)
            banks = 2 if s >= GROUPS - SPLIT_GROUPS else 1
            heads = 2 * HEADS // banks
            for j in range(tiles):
                for b in range(banks):
                    copy = nc.vector.tensor_copy if vector_helps and (j + b) % 2 == 1 else nc.scalar.copy
                    copy(
                        out=result[:, b * heads : (b + 1) * heads, j, :],
                        in_=acc[s, j, b][:].rearrange("p (a d) -> p a d", d=HEAD_DIM),
                    )
            for kv, out in enumerate((out_0, out_1)):
                nc.sync.dma_start(
                    out=out[layer][:, first_row : first_row + P * tiles].rearrange("n (p j) d -> p n (j d)", j=tiles),
                    in_=result[:, kv * HEADS : (kv + 1) * HEADS].rearrange("p n j d -> p n (j d)"),
                )

        def transpose_weights(layer):
            for kv in range(2):
                w_ps[layer, kv] = psum_w.tile([P, HEADS, HALVES, P], F32, name="w_ps")
                for n in range(HEADS):
                    for u in range(HALVES):
                        nc.tensor.transpose(
                            out=w_ps[layer, kv][:, n, u, :],
                            in_=w_raw[layer][:, kv, n].bitcast(F32)[:, u * P : (u + 1) * P], identity=ident[:],
                        )

        def regroup_weights(layer):
            copy = nc.scalar.copy if layer == 0 else nc.vector.tensor_copy
            w_grouped[layer] = weights.tile([P, 2, HEADS * FEATURES], BF16, name="w_grouped", bufs=2, align_bytes=64)
            for kv in range(2):
                copy(
                    out=w_grouped[layer][:, kv].bitcast(F32).rearrange("p (n d u) -> p n d u", n=HEADS, u=HALVES),
                    in_=w_ps[layer, kv][:].rearrange("p n u d -> p n d u"),
                )

        def quantise_weights(layer):
            w_codes[layer] = weights.tile([P, OUT_COLS], U32, name="w_codes", align_bytes=64)
            w_scales[layer] = weights.tile([P, OUT_COLS], U8, name="w_scales", align_bytes=64)
            nc.vector.quantize_mx(
                out=w_codes[layer][:].bitcast(FP8X4), scales=w_scales[layer][:],
                in_=w_grouped[layer][:].rearrange("p a c -> p (a c)"),
            )

        fuse(0)
        spread_first_gain()
        for s in range(GROUPS + 4):
            if s - 1 in FIRST_GROUPS:
                transpose_weights(FIRST_GROUPS[s - 1])
            if s - 3 in FIRST_GROUPS:
                quantise_weights(FIRST_GROUPS[s - 3])
            if 0 <= s - 3 < GROUPS:
                quantise_and_project(s - 3)
            if 0 <= s - 4:
                copy_out_and_store(s - 4, vector_helps=s + 1 >= GROUPS)
            if s < GROUPS:
                square(s)
            if 0 <= s - 2 < GROUPS:
                regroup(s - 2)
            if s < GROUPS:
                finish_statistics(s)
            if 0 <= s - 1 < GROUPS:
                normalise_and_transpose(s - 1)
            if s + 1 < GROUPS:
                fuse(s + 1)
            if s - 1 in FIRST_GROUPS:
                regroup_weights(FIRST_GROUPS[s - 1])
